import numpy as np
import ml_dtypes

BF16 = ml_dtypes.bfloat16


def bf(x):
    return np.asarray(x, np.float32).astype(BF16)


def f32(x):
    return np.asarray(x, np.float32)


def f64(x):
    return np.asarray(x).astype(np.float64)


def striped(idx):
    return np.tile(idx.reshape(-1, 16).T, (8, 1))


F, C, S, P, N, NB = 4, 256, 2048, 1024, 4096, 26
GAIN_INTRA = 4.0
GAIN_INTER = 2.0


def frame_mix():
    a = np.eye(F) + np.eye(F, k=1) + np.eye(F, k=-1)
    d = 1.0 / np.sqrt(a.sum(-1))
    return a * d[:, None] * d[None, :]


def setup_inputs():
    x = f32(np.random.standard_normal((F, C, S)))
    up = np.triu(np.random.random((P, P)) < NB / P, 1)
    adj = bf(up + up.T + np.eye(P))
    w_intra = bf(GAIN_INTRA * np.random.standard_normal((C, C)) / np.sqrt(C))
    w_inter = bf(GAIN_INTER * np.random.standard_normal((C, C)) / np.sqrt(C))
    idx = np.concatenate([np.random.permutation(S)[:P] for _ in range(F)])
    return {"x": x, "adj": adj, "w_intra": w_intra, "w_inter": w_inter, "offs": striped(idx)}


def reference(x, adj, w_intra, w_inter, offs):
    idx = offs[:16].T.reshape(-1)
    pieces = idx.reshape(F, P)
    xs = f64(x)
    a = f64(adj)
    dinv = 1.0 / np.sqrt(a.sum(-1))
    asp = a * dinv[:, None] * dinv[None, :]
    picked = np.stack([xs[t][:, pieces[t]] for t in range(F)])
    agg = picked @ asp.T
    h = np.maximum(np.einsum('kc,tkn->tcn', f64(w_intra), agg), 0.0)
    y = np.einsum('tu,ukn->tkn', frame_mix(), h)
    res = np.maximum(np.einsum('kc,tkn->tcn', f64(w_inter), y), 0.0)
    return res.transpose(1, 0, 2).reshape(C, N)

@@ -1,0 +1,158 @@
+import math
+
+import concourse.mybir as mybir
+from concourse.masks import make_identity
+
+F32 = mybir.dt.float32
+BF16 = mybir.dt.bfloat16
+U16 = mybir.dt.uint16
+ACT = mybir.ActivationFunctionType
+ALU = mybir.AluOpType
+
+FRAMES = 4
+CHANNELS = 256
+NODES = 2048
+PLACES = 1024
+PART = 128
+BANK = 512
+CHANNEL_BLOCKS = CHANNELS // PART
+PLACE_BLOCKS = PLACES // PART
+PLACE_HALVES = PLACES // BANK
+LIST_COLUMNS = PLACES // 16
+FRAME_DEGREE = (2, 3, 3, 2)
+
+FLOPS = 2 * FRAMES * (PLACES * PLACES * CHANNELS + 2 * CHANNELS * CHANNELS * PLACES)
+
+
+def neighbours(t):
+    return [u for u in (t - 1, t, t + 1) if 0 <= u < FRAMES]
+
+
+def block(i):
+    return slice(i * PART, (i + 1) * PART)
+
+
+def half(i):
+    return slice(i * BANK, (i + 1) * BANK)
+
+
+def tile_differentialgcnblock_b_kernel(tc, x, adj, w_intra, w_inter, offs, out):
+    nc = tc.nc
+    with (
+        tc.tile_pool(name="held", bufs=1) as held,
+        tc.tile_pool(name="ring", bufs=3) as ring,
+        tc.psum_pool(name="psum", bufs=8) as psum,
+    ):
+        offsets = held.tile([PART, FRAMES * LIST_COLUMNS], U16, name="offsets")
+        nc.sync.dma_start(offsets[:], offs)
+        w_intra_sb = held.tile([PART, CHANNEL_BLOCKS, CHANNELS], BF16, name="w_intra_sb")
+        nc.sync.dma_start(w_intra_sb[:], w_intra.rearrange("(kb p) c -> p kb c", p=PART))
+        x_sb = [[held.tile([PART, NODES], F32, name=f"x{t}_{kb}") for kb in range(CHANNEL_BLOCKS)] for t in range(FRAMES)]
+        adj_sb = [held.tile([PART, PLACES], BF16, name=f"adj{mb}") for mb in range(PLACE_BLOCKS)]
+        w_inter_sb = held.tile([PART, CHANNEL_BLOCKS, CHANNELS], BF16, name="w_inter_sb")
+
+        def load_frame(t):
+            for kb in range(CHANNEL_BLOCKS):
+                nc.sync.dma_start(x_sb[t][kb][:], x[t, block(kb), :])
+
+        load_frame(0)
+        for mb in range(PLACE_BLOCKS):
+            nc.sync.dma_start(adj_sb[mb][:], adj[block(mb), :])
+        nc.sync.dma_start(w_inter_sb[:], w_inter.rearrange("(kb p) c -> p kb c", p=PART))
+        for t in range(1, FRAMES):
+            load_frame(t)
+
+        degree = held.tile([PART, PLACE_BLOCKS], F32, name="degree")
+        for mb in range(PLACE_BLOCKS):
+            nc.vector.reduce_sum(degree[:, mb : mb + 1], adj_sb[mb][:], axis=mybir.AxisListType.X)
+        root = held.tile([PART, PLACE_BLOCKS], F32, name="root")
+        nc.scalar.activation(root[:], degree[:], ACT.Sqrt)
+        dinv = held.tile([PART, PLACE_BLOCKS], F32, name="dinv")
+        nc.vector.reciprocal(dinv[:], root[:])
+
+        picked_bf = [[held.tile([PART, PLACES], BF16, name=f"picked_bf{t}_{kb}") for kb in range(CHANNEL_BLOCKS)] for t in range(FRAMES)]
+        q_t = [held.tile([PART, PLACE_BLOCKS, CHANNELS], BF16, name=f"q_t{t}") for t in range(FRAMES)]
+        h = [[held.tile([PART, PLACES], F32, name=f"h{t}_{cb}") for cb in range(CHANNEL_BLOCKS)] for t in range(FRAMES)]
+        y = [[held.tile([PART, PLACES], BF16, name=f"y{t}_{cb}") for cb in range(CHANNEL_BLOCKS)] for t in range(FRAMES)]
+
+        def pick_and_project(t):
+            for kb in range(CHANNEL_BLOCKS):
+                picked = ring.tile([PART, PLACES], F32, name="picked")
+                frame_list = offsets[:, t * LIST_COLUMNS : (t + 1) * LIST_COLUMNS]
+                nc.scalar.activation(picked[:], x_sb[t][kb][:].indirect(frame_list), ACT.Copy)
+                nc.vector.tensor_copy(picked_bf[t][kb][:], picked[:])
+            for mb in range(PLACE_BLOCKS):
+                q_ps = psum.tile([PART, BANK], F32, name="q_ps", tag="bank")
+                for kb in range(CHANNEL_BLOCKS):
+                    nc.tensor.matmul(
+                        q_ps[:, :CHANNELS],
+                        lhsT=picked_bf[t][kb][:, block(mb)],
+                        rhs=w_intra_sb[:, kb, :],
+                        start=kb == 0,
+                        stop=kb == CHANNEL_BLOCKS - 1,
+                    )
+                nc.vector.tensor_scalar(q_t[t][:, mb, :], q_ps[:, :CHANNELS], dinv[:, mb : mb + 1], None, ALU.mult)
+
+        def aggregate(t, nh):
+            for cb in range(CHANNEL_BLOCKS):
+                z_ps = psum.tile([PART, BANK], F32, name="z_ps", tag="bank")
+                for mb in range(PLACE_BLOCKS):
+                    nc.tensor.matmul(
+                        z_ps[:],
+                        lhsT=q_t[t][:, mb, block(cb)],
+                        rhs=adj_sb[mb][:, half(nh)],
+                        start=mb == 0,
+                        stop=mb == PLACE_BLOCKS - 1,
+                    )
+                nc.scalar.activation(h[t][cb][:, half(nh)], z_ps[:], ACT.Relu, scale=1.0 / math.sqrt(FRAME_DEGREE[t]))
+
+        def mix(t, nh):
+            frames = neighbours(t)
+            for cb in range(CHANNEL_BLOCKS):
+                partial = h[frames[0]][cb][:, half(nh)]
+                for u in frames[1:-1]:
+                    longer = ring.tile([PART, BANK], F32, name="longer")
+                    nc.vector.tensor_tensor(longer[:], partial, h[u][cb][:, half(nh)], ALU.add)
+                    partial = longer[:]
+                nc.vector.tensor_tensor(y[t][cb][:, half(nh)], partial, h[frames[-1]][cb][:, half(nh)], ALU.add)
+
+        def project_out(t, nh):
+            for cb in range(CHANNEL_BLOCKS):
+                o_ps = psum.tile([PART, BANK], F32, name="o_ps", tag="bank")
+                for kb in range(CHANNEL_BLOCKS):
+                    nc.tensor.matmul(
+                        o_ps[:],
+                        lhsT=w_inter_sb[:, kb, block(cb)],
+                        rhs=y[t][kb][:, half(nh)],
+                        start=kb == 0,
+                        stop=kb == CHANNEL_BLOCKS - 1,
+                    )
+                result = ring.tile([PART, BANK], F32, name="result")
+                nc.vector.scalar_tensor_tensor(
+                    result[:], o_ps[:], 0.0, dinv_row[FRAME_DEGREE[t]][:, half(nh)], ALU.max, ALU.mult
+                )
+                nc.sync.dma_start(out[block(cb), t * PLACES + nh * BANK : t * PLACES + (nh + 1) * BANK], result[:])
+
+        pick_and_project(0)
+
+        identity = held.tile([PART, PART], F32, name="identity")
+        make_identity(nc, identity[:])
+        spread = held.tile([PART, PLACE_BLOCKS, PART], F32, name="spread")
+        nc.vector.tensor_copy(spread[:], dinv[:].unsqueeze(2).to_broadcast([PART, PLACE_BLOCKS, PART]))
+        dinv_row = {d: held.tile([PART, PLACES], F32, name=f"dinv_row{d}") for d in sorted(set(FRAME_DEGREE))}
+        for nh in range(PLACE_HALVES):
+            row_ps = psum.tile([PART, BANK], F32, name="row_ps", tag="bank")
+            for i in range(BANK // PART):
+                nc.tensor.transpose(row_ps[:, block(i)], spread[:, nh * (BANK // PART) + i, :], identity[:])
+            for d in dinv_row:
+                nc.vector.tensor_scalar(dinv_row[d][:, half(nh)], row_ps[:], 1.0 / math.sqrt(d), None, ALU.mult)
+
+        for t in range(FRAMES):
+            if t + 1 < FRAMES:
+                pick_and_project(t + 1)
+            for nh in range(PLACE_HALVES):
+                aggregate(t, nh)
+                for u in range(FRAMES):
+                    if neighbours(u)[-1] == t:
+                        mix(u, nh)
+                        project_out(u, nh)

@@ -16,9 +16,10 @@ PLACES = 1024
 PART = 128
 BANK = 512
 CHANNEL_BLOCKS = CHANNELS // PART
-PLACE_BLOCKS = PLACES // PART
 PLACE_HALVES = PLACES // BANK
-LIST_COLUMNS = PLACES // 16
+PAIRS = PLACES // (2 * PART)
+PAIRS_IN_HALF = PAIRS // PLACE_HALVES
+PIECE_COLUMNS = BANK // 16
 FRAME_DEGREE = (2, 3, 3, 2)
 
 FLOPS = 2 * FRAMES * (PLACES * PLACES * CHANNELS + 2 * CHANNELS * CHANNELS * PLACES)
@@ -28,27 +29,30 @@ def neighbours(t):
     return [u for u in (t - 1, t, t + 1) if 0 <= u < FRAMES]
 
 
+INNER = (1, 2)
+
+
 def block(i):
     return slice(i * PART, (i + 1) * PART)
-
-
-def half(i):
-    return slice(i * BANK, (i + 1) * BANK)
 
 
 def tile_differentialgcnblock_b_kernel(tc, x, adj, w_intra, w_inter, offs, out):
     nc = tc.nc
     with (
         tc.tile_pool(name="held", bufs=1) as held,
-        tc.tile_pool(name="ring", bufs=3) as ring,
+        tc.tile_pool(name="ring", bufs=4) as ring,
         tc.psum_pool(name="psum", bufs=8) as psum,
     ):
-        offsets = held.tile([PART, FRAMES * LIST_COLUMNS], U16, name="offsets")
+        one = held.tile([PART, 1], F32, name="one")
+        nc.vector.memset(one[:], 1.0)
+        root_of_one = held.tile([PART, 1], F32, name="root_of_one")
+        nc.scalar.activation(root_of_one[:], one[:], ACT.Sqrt)
+
+        offsets = held.tile([PART, FRAMES * PLACE_HALVES * PIECE_COLUMNS], U16, name="offsets")
         nc.sync.dma_start(offsets[:], offs)
-        w_intra_sb = held.tile([PART, CHANNEL_BLOCKS, CHANNELS], BF16, name="w_intra_sb")
-        nc.sync.dma_start(w_intra_sb[:], w_intra.rearrange("(kb p) c -> p kb c", p=PART))
         x_sb = [[held.tile([PART, NODES], F32, name=f"x{t}_{kb}") for kb in range(CHANNEL_BLOCKS)] for t in range(FRAMES)]
-        adj_sb = [held.tile([PART, PLACES], BF16, name=f"adj{mb}") for mb in range(PLACE_BLOCKS)]
+        adj_sb = [held.tile([PART, 2, PLACES], BF16, name=f"adj{pair}") for pair in range(PAIRS)]
+        w_intra_sb = held.tile([PART, CHANNEL_BLOCKS, CHANNELS], BF16, name="w_intra_sb")
         w_inter_sb = held.tile([PART, CHANNEL_BLOCKS, CHANNELS], BF16, name="w_inter_sb")
 
         def load_frame(t):
@@ -56,65 +60,76 @@ def tile_differentialgcnblock_b_kernel(tc, x, adj, w_intra, w_inter, offs, out):
                 nc.sync.dma_start(x_sb[t][kb][:], x[t, block(kb), :])
 
         load_frame(0)
-        for mb in range(PLACE_BLOCKS):
-            nc.sync.dma_start(adj_sb[mb][:], adj[block(mb), :])
+        nc.sync.dma_start(w_intra_sb[:], w_intra.rearrange("(kb p) c -> p kb c", p=PART))
+        for pair in range(PAIRS):
+            rows = slice(pair * 2 * PART, (pair + 1) * 2 * PART)
+            nc.sync.dma_start(adj_sb[pair][:], adj[rows, :].rearrange("(i p) n -> p i n", p=PART))
         nc.sync.dma_start(w_inter_sb[:], w_inter.rearrange("(kb p) c -> p kb c", p=PART))
         for t in range(1, FRAMES):
             load_frame(t)
 
-        degree = held.tile([PART, PLACE_BLOCKS], F32, name="degree")
-        for mb in range(PLACE_BLOCKS):
-            nc.vector.reduce_sum(degree[:, mb : mb + 1], adj_sb[mb][:], axis=mybir.AxisListType.X)
-        root = held.tile([PART, PLACE_BLOCKS], F32, name="root")
-        nc.scalar.activation(root[:], degree[:], ACT.Sqrt)
-        dinv = held.tile([PART, PLACE_BLOCKS], F32, name="dinv")
-        nc.vector.reciprocal(dinv[:], root[:])
+        picked_bf = [[[held.tile([PART, BANK], BF16, name=f"picked_bf{t}_{kb}_{mh}") for mh in range(PLACE_HALVES)] for kb in range(CHANNEL_BLOCKS)] for t in range(FRAMES)]
+        q_t = [[held.tile([PART, 2, CHANNELS], BF16, name=f"q_t{t}_{pair}") for pair in range(PAIRS)] for t in range(FRAMES)]
+        h = [[[held.tile([PART, BANK], F32, name=f"h{t}_{cb}_{nh}") for nh in range(PLACE_HALVES)] for cb in range(CHANNEL_BLOCKS)] for t in range(FRAMES)]
+        inner = [[held.tile([PART, BANK], F32, name=f"inner{cb}_{nh}") for nh in range(PLACE_HALVES)] for cb in range(CHANNEL_BLOCKS)]
+        y = [[[held.tile([PART, BANK], BF16, name=f"y{t}_{cb}_{nh}") for nh in range(PLACE_HALVES)] for cb in range(CHANNEL_BLOCKS)] for t in range(FRAMES)]
 
-        picked_bf = [[held.tile([PART, PLACES], BF16, name=f"picked_bf{t}_{kb}") for kb in range(CHANNEL_BLOCKS)] for t in range(FRAMES)]
-        q_t = [held.tile([PART, PLACE_BLOCKS, CHANNELS], BF16, name=f"q_t{t}") for t in range(FRAMES)]
-        h = [[held.tile([PART, PLACES], F32, name=f"h{t}_{cb}") for cb in range(CHANNEL_BLOCKS)] for t in range(FRAMES)]
-        y = [[held.tile([PART, PLACES], BF16, name=f"y{t}_{cb}") for cb in range(CHANNEL_BLOCKS)] for t in range(FRAMES)]
-
-        def pick_and_project(t):
-            for kb in range(CHANNEL_BLOCKS):
-                picked = ring.tile([PART, PLACES], F32, name="picked")
-                frame_list = offsets[:, t * LIST_COLUMNS : (t + 1) * LIST_COLUMNS]
-                nc.scalar.activation(picked[:], x_sb[t][kb][:].indirect(frame_list), ACT.Copy)
-                nc.vector.tensor_copy(picked_bf[t][kb][:], picked[:])
-            for mb in range(PLACE_BLOCKS):
-                q_ps = psum.tile([PART, BANK], F32, name="q_ps", tag="bank")
+        def pick(t):
+            for mh in range(PLACE_HALVES):
+                first_column = (t * PLACE_HALVES + mh) * PIECE_COLUMNS
+                piece = offsets[:, first_column : first_column + PIECE_COLUMNS]
                 for kb in range(CHANNEL_BLOCKS):
-                    nc.tensor.matmul(
-                        q_ps[:, :CHANNELS],
-                        lhsT=picked_bf[t][kb][:, block(mb)],
-                        rhs=w_intra_sb[:, kb, :],
-                        start=kb == 0,
-                        stop=kb == CHANNEL_BLOCKS - 1,
+                    picked = ring.tile([PART, BANK], F32, name="picked")
+                    nc.scalar.activation(picked[:], x_sb[t][kb][:].indirect(piece), ACT.Copy)
+                    nc.vector.tensor_copy(picked_bf[t][kb][mh][:], picked[:])
+
+        def project(t):
+            for pair in range(PAIRS):
+                mh, j = divmod(pair, PAIRS_IN_HALF)
+                q_ps = psum.tile([PART, 2, CHANNELS], F32, name="q_ps", tag="bank")
+                for i in range(2):
+                    for kb in range(CHANNEL_BLOCKS):
+                        nc.tensor.matmul(
+                            q_ps[:, i, :],
+                            lhsT=picked_bf[t][kb][mh][:, block(2 * j + i)],
+                            rhs=w_intra_sb[:, kb, :],
+                            start=kb == 0,
+                            stop=kb == CHANNEL_BLOCKS - 1,
+                        )
+                if pair % 2 == 0:
+                    for i in range(2):
+                        nc.scalar.activation(q_t[t][pair][:, i, :], q_ps[:, i, :], ACT.Identity, scale=dinv[pair][:, i : i + 1])
+                else:
+                    nc.vector.tensor_tensor(
+                        q_t[t][pair][:], q_ps[:], dinv[pair][:].unsqueeze(2).to_broadcast([PART, 2, CHANNELS]), ALU.mult
                     )
-                nc.vector.tensor_scalar(q_t[t][:, mb, :], q_ps[:, :CHANNELS], dinv[:, mb : mb + 1], None, ALU.mult)
 
         def aggregate(t, nh):
-            for cb in range(CHANNEL_BLOCKS):
-                z_ps = psum.tile([PART, BANK], F32, name="z_ps", tag="bank")
-                for mb in range(PLACE_BLOCKS):
-                    nc.tensor.matmul(
-                        z_ps[:],
-                        lhsT=q_t[t][:, mb, block(cb)],
-                        rhs=adj_sb[mb][:, half(nh)],
-                        start=mb == 0,
-                        stop=mb == PLACE_BLOCKS - 1,
-                    )
-                nc.scalar.activation(h[t][cb][:, half(nh)], z_ps[:], ACT.Relu, scale=1.0 / math.sqrt(FRAME_DEGREE[t]))
+            g = 1.0 / math.sqrt(FRAME_DEGREE[t])
+            z_ps = [psum.tile([PART, BANK], F32, name=f"z_ps{cb}", tag="bank") for cb in range(CHANNEL_BLOCKS)]
+            for pair in range(PAIRS):
+                for i in range(2):
+                    for cb in range(CHANNEL_BLOCKS):
+                        nc.tensor.matmul(
+                            z_ps[cb][:],
+                            lhsT=q_t[t][pair][:, i, block(cb)],
+                            rhs=adj_sb[pair][:, i, nh * BANK : (nh + 1) * BANK],
+                            start=pair == 0 and i == 0,
+                            stop=pair == PAIRS - 1 and i == 1,
+                        )
+            nc.scalar.activation(h[t][0][nh][:], z_ps[0][:], ACT.Relu, scale=g)
+            nc.vector.tensor_scalar(h[t][1][nh][:], z_ps[1][:], g, 0.0, ALU.mult, ALU.max)
 
         def mix(t, nh):
-            frames = neighbours(t)
             for cb in range(CHANNEL_BLOCKS):
-                partial = h[frames[0]][cb][:, half(nh)]
-                for u in frames[1:-1]:
-                    longer = ring.tile([PART, BANK], F32, name="longer")
-                    nc.vector.tensor_tensor(longer[:], partial, h[u][cb][:, half(nh)], ALU.add)
-                    partial = longer[:]
-                nc.vector.tensor_tensor(y[t][cb][:, half(nh)], partial, h[frames[-1]][cb][:, half(nh)], ALU.add)
+                if t == INNER[0]:
+                    nc.vector.tensor_tensor(inner[cb][nh][:], h[INNER[0]][cb][nh][:], h[INNER[1]][cb][nh][:], ALU.add)
+                if t in INNER:
+                    (outer,) = [u for u in neighbours(t) if u not in INNER]
+                    nc.vector.tensor_tensor(y[t][cb][nh][:], inner[cb][nh][:], h[outer][cb][nh][:], ALU.add)
+                else:
+                    a, b = neighbours(t)
+                    nc.vector.tensor_tensor(y[t][cb][nh][:], h[a][cb][nh][:], h[b][cb][nh][:], ALU.add)
 
         def project_out(t, nh):
             for cb in range(CHANNEL_BLOCKS):
@@ -123,35 +138,57 @@ def tile_differentialgcnblock_b_kernel(tc, x, adj, w_intra, w_inter, offs, out):
                     nc.tensor.matmul(
                         o_ps[:],
                         lhsT=w_inter_sb[:, kb, block(cb)],
-                        rhs=y[t][kb][:, half(nh)],
+                        rhs=y[t][kb][nh][:],
                         start=kb == 0,
                         stop=kb == CHANNEL_BLOCKS - 1,
                     )
                 result = ring.tile([PART, BANK], F32, name="result")
-                nc.vector.scalar_tensor_tensor(
-                    result[:], o_ps[:], 0.0, dinv_row[FRAME_DEGREE[t]][:, half(nh)], ALU.max, ALU.mult
-                )
-                nc.sync.dma_start(out[block(cb), t * PLACES + nh * BANK : t * PLACES + (nh + 1) * BANK], result[:])
+                nc.vector.scalar_tensor_tensor(result[:], o_ps[:], 0.0, dinv_row[FRAME_DEGREE[t]][nh][:], ALU.max, ALU.mult)
+                first_column = t * PLACES + nh * BANK
+                nc.sync.dma_start(out[block(cb), first_column : first_column + BANK], result[:])
 
-        pick_and_project(0)
+        pick(0)
+
+        dinv = []
+        for pair in range(PAIRS):
+            degree = held.tile([PART, 2], F32, name=f"degree{pair}")
+            for i in range(2):
+                unused = ring.tile([PART, PLACES], BF16, name="unused")
+                nc.vector.tensor_scalar(
+                    unused[:], adj_sb[pair][:, i, :], 1.0, None, ALU.mult, ALU.add, accum_out=degree[:, i : i + 1]
+                )
+            root = held.tile([PART, 2], F32, name=f"root{pair}")
+            nc.scalar.activation(root[:], degree[:], ACT.Sqrt)
+            dinv.append(held.tile([PART, 2], F32, name=f"dinv{pair}"))
+            nc.vector.reciprocal(dinv[pair][:], root[:])
+
+        project(0)
 
         identity = held.tile([PART, PART], F32, name="identity")
         make_identity(nc, identity[:])
-        spread = held.tile([PART, PLACE_BLOCKS, PART], F32, name="spread")
-        nc.vector.tensor_copy(spread[:], dinv[:].unsqueeze(2).to_broadcast([PART, PLACE_BLOCKS, PART]))
-        dinv_row = {d: held.tile([PART, PLACES], F32, name=f"dinv_row{d}") for d in sorted(set(FRAME_DEGREE))}
-        for nh in range(PLACE_HALVES):
-            row_ps = psum.tile([PART, BANK], F32, name="row_ps", tag="bank")
-            for i in range(BANK // PART):
-                nc.tensor.transpose(row_ps[:, block(i)], spread[:, nh * (BANK // PART) + i, :], identity[:])
-            for d in dinv_row:
-                nc.vector.tensor_scalar(dinv_row[d][:, half(nh)], row_ps[:], 1.0 / math.sqrt(d), None, ALU.mult)
+        dinv_row = {d: [held.tile([PART, BANK], F32, name=f"dinv_row{d}_{nh}") for nh in range(PLACE_HALVES)] for d in sorted(set(FRAME_DEGREE))}
+
+        def spread_dinv():
+            for nh in range(PLACE_HALVES):
+                row_ps = psum.tile([PART, BANK], F32, name="row_ps", tag="bank")
+                for j in range(PAIRS_IN_HALF):
+                    spread = ring.tile([PART, 2, PART], F32, name="spread")
+                    nc.gpsimd.tensor_copy(spread[:], dinv[nh * PAIRS_IN_HALF + j][:].unsqueeze(2).to_broadcast([PART, 2, PART]))
+                    for i in range(2):
+                        nc.tensor.transpose(row_ps[:, block(2 * j + i)], spread[:, i, :], identity[:])
+                for d in dinv_row:
+                    nc.vector.tensor_scalar(dinv_row[d][nh][:], row_ps[:], 1.0 / math.sqrt(d), None, ALU.mult)
 
         for t in range(FRAMES):
             if t + 1 < FRAMES:
-                pick_and_project(t + 1)
+                pick(t + 1)
             for nh in range(PLACE_HALVES):
                 aggregate(t, nh)
+            if t + 1 < FRAMES:
+                project(t + 1)
+            if t == 0:
+                spread_dinv()
+            for nh in range(PLACE_HALVES):
                 for u in range(FRAMES):
                     if neighbours(u)[-1] == t:
                         mix(u, nh)

@@ -19,7 +19,8 @@ CHANNEL_BLOCKS = CHANNELS // PART
 PLACE_HALVES = PLACES // BANK
 PAIRS = PLACES // (2 * PART)
 PAIRS_IN_HALF = PAIRS // PLACE_HALVES
-PIECE_COLUMNS = BANK // 16
+PAIR_PLACES = 2 * PART
+PIECE_COLUMNS = PAIR_PLACES // 16
 FRAME_DEGREE = (2, 3, 3, 2)
 
 FLOPS = 2 * FRAMES * (PLACES * PLACES * CHANNELS + 2 * CHANNELS * CHANNELS * PLACES)
@@ -48,7 +49,7 @@ def tile_differentialgcnblock_b_kernel(tc, x, adj, w_intra, w_inter, offs, out):
         root_of_one = held.tile([PART, 1], F32, name="root_of_one")
         nc.scalar.activation(root_of_one[:], one[:], ACT.Sqrt)
 
-        offsets = held.tile([PART, FRAMES * PLACE_HALVES * PIECE_COLUMNS], U16, name="offsets")
+        offsets = held.tile([PART, FRAMES * PAIRS * PIECE_COLUMNS], U16, name="offsets")
         nc.sync.dma_start(offsets[:], offs)
         x_sb = [[held.tile([PART, NODES], F32, name=f"x{t}_{kb}") for kb in range(CHANNEL_BLOCKS)] for t in range(FRAMES)]
         adj_sb = [held.tile([PART, 2, PLACES], BF16, name=f"adj{pair}") for pair in range(PAIRS)]
@@ -62,50 +63,44 @@ def tile_differentialgcnblock_b_kernel(tc, x, adj, w_intra, w_inter, offs, out):
         load_frame(0)
         nc.sync.dma_start(w_intra_sb[:], w_intra.rearrange("(kb p) c -> p kb c", p=PART))
         for pair in range(PAIRS):
-            rows = slice(pair * 2 * PART, (pair + 1) * 2 * PART)
+            rows = slice(pair * PAIR_PLACES, (pair + 1) * PAIR_PLACES)
             nc.sync.dma_start(adj_sb[pair][:], adj[rows, :].rearrange("(i p) n -> p i n", p=PART))
+        load_frame(1)
         nc.sync.dma_start(w_inter_sb[:], w_inter.rearrange("(kb p) c -> p kb c", p=PART))
-        for t in range(1, FRAMES):
-            load_frame(t)
+        load_frame(2)
+        load_frame(3)
 
-        picked_bf = [[[held.tile([PART, BANK], BF16, name=f"picked_bf{t}_{kb}_{mh}") for mh in range(PLACE_HALVES)] for kb in range(CHANNEL_BLOCKS)] for t in range(FRAMES)]
+        picked_bf = [[[held.tile([PART, PAIR_PLACES], BF16, name=f"picked_bf{t}_{kb}_{pair}") for pair in range(PAIRS)] for kb in range(CHANNEL_BLOCKS)] for t in range(FRAMES)]
         q_t = [[held.tile([PART, 2, CHANNELS], BF16, name=f"q_t{t}_{pair}") for pair in range(PAIRS)] for t in range(FRAMES)]
         h = [[[held.tile([PART, BANK], F32, name=f"h{t}_{cb}_{nh}") for nh in range(PLACE_HALVES)] for cb in range(CHANNEL_BLOCKS)] for t in range(FRAMES)]
         inner = [[held.tile([PART, BANK], F32, name=f"inner{cb}_{nh}") for nh in range(PLACE_HALVES)] for cb in range(CHANNEL_BLOCKS)]
         y = [[[held.tile([PART, BANK], BF16, name=f"y{t}_{cb}_{nh}") for nh in range(PLACE_HALVES)] for cb in range(CHANNEL_BLOCKS)] for t in range(FRAMES)]
 
         def pick(t):
-            for mh in range(PLACE_HALVES):
-                first_column = (t * PLACE_HALVES + mh) * PIECE_COLUMNS
+            for pair in range(PAIRS):
+                first_column = (t * PAIRS + pair) * PIECE_COLUMNS
                 piece = offsets[:, first_column : first_column + PIECE_COLUMNS]
                 for kb in range(CHANNEL_BLOCKS):
-                    picked = ring.tile([PART, BANK], F32, name="picked")
+                    picked = ring.tile([PART, PAIR_PLACES], F32, name="picked", bufs=8)
                     nc.scalar.activation(picked[:], x_sb[t][kb][:].indirect(piece), ACT.Copy)
-                    nc.vector.tensor_copy(picked_bf[t][kb][mh][:], picked[:])
+                    nc.vector.tensor_copy(picked_bf[t][kb][pair][:], picked[:])
 
         def project(t):
             for pair in range(PAIRS):
-                mh, j = divmod(pair, PAIRS_IN_HALF)
                 q_ps = psum.tile([PART, 2, CHANNELS], F32, name="q_ps", tag="bank")
                 for i in range(2):
                     for kb in range(CHANNEL_BLOCKS):
                         nc.tensor.matmul(
                             q_ps[:, i, :],
-                            lhsT=picked_bf[t][kb][mh][:, block(2 * j + i)],
+                            lhsT=picked_bf[t][kb][pair][:, block(i)],
                             rhs=w_intra_sb[:, kb, :],
                             start=kb == 0,
                             stop=kb == CHANNEL_BLOCKS - 1,
                         )
-                if pair % 2 == 0:
-                    for i in range(2):
-                        nc.scalar.activation(q_t[t][pair][:, i, :], q_ps[:, i, :], ACT.Identity, scale=dinv[pair][:, i : i + 1])
-                else:
-                    nc.vector.tensor_tensor(
-                        q_t[t][pair][:], q_ps[:], dinv[pair][:].unsqueeze(2).to_broadcast([PART, 2, CHANNELS]), ALU.mult
-                    )
+                for i in range(2):
+                    nc.scalar.activation(q_t[t][pair][:, i, :], q_ps[:, i, :], ACT.Identity, scale=dinv[pair][:, i : i + 1])
 
         def aggregate(t, nh):
-            g = 1.0 / math.sqrt(FRAME_DEGREE[t])
             z_ps = [psum.tile([PART, BANK], F32, name=f"z_ps{cb}", tag="bank") for cb in range(CHANNEL_BLOCKS)]
             for pair in range(PAIRS):
                 for i in range(2):
@@ -117,21 +112,23 @@ def tile_differentialgcnblock_b_kernel(tc, x, adj, w_intra, w_inter, offs, out):
                             start=pair == 0 and i == 0,
                             stop=pair == PAIRS - 1 and i == 1,
                         )
-            nc.scalar.activation(h[t][0][nh][:], z_ps[0][:], ACT.Relu, scale=g)
-            nc.vector.tensor_scalar(h[t][1][nh][:], z_ps[1][:], g, 0.0, ALU.mult, ALU.max)
+            for cb in range(CHANNEL_BLOCKS):
+                nc.vector.scalar_tensor_tensor(h[t][cb][nh][:], z_ps[cb][:], 0.0, dinv_row[FRAME_DEGREE[t]][nh][:], ALU.max, ALU.mult)
 
         def mix(t, nh):
+            engine = nc.vector if t % 2 == 0 else nc.gpsimd
             for cb in range(CHANNEL_BLOCKS):
                 if t == INNER[0]:
-                    nc.vector.tensor_tensor(inner[cb][nh][:], h[INNER[0]][cb][nh][:], h[INNER[1]][cb][nh][:], ALU.add)
+                    engine.tensor_tensor(inner[cb][nh][:], h[INNER[0]][cb][nh][:], h[INNER[1]][cb][nh][:], ALU.add)
                 if t in INNER:
                     (outer,) = [u for u in neighbours(t) if u not in INNER]
-                    nc.vector.tensor_tensor(y[t][cb][nh][:], inner[cb][nh][:], h[outer][cb][nh][:], ALU.add)
+                    engine.tensor_tensor(y[t][cb][nh][:], inner[cb][nh][:], h[outer][cb][nh][:], ALU.add)
                 else:
                     a, b = neighbours(t)
-                    nc.vector.tensor_tensor(y[t][cb][nh][:], h[a][cb][nh][:], h[b][cb][nh][:], ALU.add)
+                    engine.tensor_tensor(y[t][cb][nh][:], h[a][cb][nh][:], h[b][cb][nh][:], ALU.add)
 
         def project_out(t, nh):
+            g = 1.0 / math.sqrt(FRAME_DEGREE[t])
             for cb in range(CHANNEL_BLOCKS):
                 o_ps = psum.tile([PART, BANK], F32, name="o_ps", tag="bank")
                 for kb in range(CHANNEL_BLOCKS):
@@ -143,7 +140,10 @@ def tile_differentialgcnblock_b_kernel(tc, x, adj, w_intra, w_inter, offs, out):
                         stop=kb == CHANNEL_BLOCKS - 1,
                     )
                 result = ring.tile([PART, BANK], F32, name="result")
-                nc.vector.scalar_tensor_tensor(result[:], o_ps[:], 0.0, dinv_row[FRAME_DEGREE[t]][nh][:], ALU.max, ALU.mult)
+                if cb % 2 == 0:
+                    nc.scalar.activation(result[:], o_ps[:], ACT.Relu, scale=g)
+                else:
+                    nc.vector.tensor_scalar(result[:], o_ps[:], g, 0.0, ALU.mult, ALU.max)
                 first_column = t * PLACES + nh * BANK
                 nc.sync.dma_start(out[block(cb), first_column : first_column + BANK], result[:])
 
@@ -167,29 +167,29 @@ def tile_differentialgcnblock_b_kernel(tc, x, adj, w_intra, w_inter, offs, out):
         identity = held.tile([PART, PART], F32, name="identity")
         make_identity(nc, identity[:])
         dinv_row = {d: [held.tile([PART, BANK], F32, name=f"dinv_row{d}_{nh}") for nh in range(PLACE_HALVES)] for d in sorted(set(FRAME_DEGREE))}
+        for nh in range(PLACE_HALVES):
+            row_ps = psum.tile([PART, BANK], F32, name="row_ps", tag="bank")
+            for j in range(PAIRS_IN_HALF):
+                spread = ring.tile([PART, 2, PART], F32, name="spread")
+                nc.gpsimd.tensor_copy(spread[:], dinv[nh * PAIRS_IN_HALF + j][:].unsqueeze(2).to_broadcast([PART, 2, PART]))
+                for i in range(2):
+                    nc.tensor.transpose(row_ps[:, block(2 * j + i)], spread[:, i, :], identity[:])
+            for d in dinv_row:
+                nc.vector.tensor_scalar(dinv_row[d][nh][:], row_ps[:], 1.0 / math.sqrt(d), None, ALU.mult)
 
-        def spread_dinv():
-            for nh in range(PLACE_HALVES):
-                row_ps = psum.tile([PART, BANK], F32, name="row_ps", tag="bank")
-                for j in range(PAIRS_IN_HALF):
-                    spread = ring.tile([PART, 2, PART], F32, name="spread")
-                    nc.gpsimd.tensor_copy(spread[:], dinv[nh * PAIRS_IN_HALF + j][:].unsqueeze(2).to_broadcast([PART, 2, PART]))
-                    for i in range(2):
-                        nc.tensor.transpose(row_ps[:, block(2 * j + i)], spread[:, i, :], identity[:])
-                for d in dinv_row:
-                    nc.vector.tensor_scalar(dinv_row[d][nh][:], row_ps[:], 1.0 / math.sqrt(d), None, ALU.mult)
-
+        summed = []
         for t in range(FRAMES):
             if t + 1 < FRAMES:
                 pick(t + 1)
             for nh in range(PLACE_HALVES):
                 aggregate(t, nh)
-            if t + 1 < FRAMES:
-                project(t + 1)
-            if t == 0:
-                spread_dinv()
-            for nh in range(PLACE_HALVES):
-                for u in range(FRAMES):
-                    if neighbours(u)[-1] == t:
-                        mix(u, nh)
-                        project_out(u, nh)
+                summed_before = summed
+                summed = [(u, nh) for u in range(FRAMES) if neighbours(u)[-1] == t]
+                for u, uh in summed:
+                    mix(u, uh)
+                if nh == PLACE_HALVES - 1 and t + 1 < FRAMES:
+                    project(t + 1)
+                for u, uh in summed_before:
+                    project_out(u, uh)
+        for u, uh in summed:
+            project_out(u, uh)

@@ -112,6 +112,8 @@ def tile_differentialgcnblock_b_kernel(tc, x, adj, w_intra, w_inter, offs, out):
                             start=pair == 0 and i == 0,
                             stop=pair == PAIRS - 1 and i == 1,
                         )
+            if t == 0:
+                spread_dinv(nh)
             for cb in range(CHANNEL_BLOCKS):
                 nc.vector.scalar_tensor_tensor(h[t][cb][nh][:], z_ps[cb][:], 0.0, dinv_row[FRAME_DEGREE[t]][nh][:], ALU.max, ALU.mult)
 
@@ -139,7 +141,7 @@ def tile_differentialgcnblock_b_kernel(tc, x, adj, w_intra, w_inter, offs, out):
                         start=kb == 0,
                         stop=kb == CHANNEL_BLOCKS - 1,
                     )
-                result = ring.tile([PART, BANK], F32, name="result")
+                result = ring.tile([PART, BANK], F32, name="result", bufs=8)
                 if cb % 2 == 0:
                     nc.scalar.activation(result[:], o_ps[:], ACT.Relu, scale=g)
                 else:
@@ -167,7 +169,8 @@ def tile_differentialgcnblock_b_kernel(tc, x, adj, w_intra, w_inter, offs, out):
         identity = held.tile([PART, PART], F32, name="identity")
         make_identity(nc, identity[:])
         dinv_row = {d: [held.tile([PART, BANK], F32, name=f"dinv_row{d}_{nh}") for nh in range(PLACE_HALVES)] for d in sorted(set(FRAME_DEGREE))}
-        for nh in range(PLACE_HALVES):
+
+        def spread_dinv(nh):
             row_ps = psum.tile([PART, BANK], F32, name="row_ps", tag="bank")
             for j in range(PAIRS_IN_HALF):
                 spread = ring.tile([PART, 2, PART], F32, name="spread")

@@ -47,7 +47,7 @@ def tile_differentialgcnblock_b_kernel(tc, x, adj, w_intra, w_inter, offs, out):
         one = held.tile([PART, 1], F32, name="one")
         nc.vector.memset(one[:], 1.0)
         root_of_one = held.tile([PART, 1], F32, name="root_of_one")
-        nc.scalar.activation(root_of_one[:], one[:], ACT.Sqrt)
+        nc.scalar.activation(root_of_one[:], one[:], ACT.Abs_reciprocal_sqrt)
 
         offsets = held.tile([PART, FRAMES * PAIRS * PIECE_COLUMNS], U16, name="offsets")
         nc.sync.dma_start(offsets[:], offs)
@@ -118,16 +118,15 @@ def tile_differentialgcnblock_b_kernel(tc, x, adj, w_intra, w_inter, offs, out):
                 nc.vector.scalar_tensor_tensor(h[t][cb][nh][:], z_ps[cb][:], 0.0, dinv_row[FRAME_DEGREE[t]][nh][:], ALU.max, ALU.mult)
 
         def mix(t, nh):
-            engine = nc.vector if t % 2 == 0 else nc.gpsimd
             for cb in range(CHANNEL_BLOCKS):
                 if t == INNER[0]:
-                    engine.tensor_tensor(inner[cb][nh][:], h[INNER[0]][cb][nh][:], h[INNER[1]][cb][nh][:], ALU.add)
+                    nc.vector.tensor_tensor(inner[cb][nh][:], h[INNER[0]][cb][nh][:], h[INNER[1]][cb][nh][:], ALU.add)
                 if t in INNER:
                     (outer,) = [u for u in neighbours(t) if u not in INNER]
-                    engine.tensor_tensor(y[t][cb][nh][:], inner[cb][nh][:], h[outer][cb][nh][:], ALU.add)
+                    nc.vector.tensor_tensor(y[t][cb][nh][:], inner[cb][nh][:], h[outer][cb][nh][:], ALU.add)
                 else:
                     a, b = neighbours(t)
-                    engine.tensor_tensor(y[t][cb][nh][:], h[a][cb][nh][:], h[b][cb][nh][:], ALU.add)
+                    nc.vector.tensor_tensor(y[t][cb][nh][:], h[a][cb][nh][:], h[b][cb][nh][:], ALU.add)
 
         def project_out(t, nh):
             g = 1.0 / math.sqrt(FRAME_DEGREE[t])
@@ -142,10 +141,7 @@ def tile_differentialgcnblock_b_kernel(tc, x, adj, w_intra, w_inter, offs, out):
                         stop=kb == CHANNEL_BLOCKS - 1,
                     )
                 result = ring.tile([PART, BANK], F32, name="result", bufs=8)
-                if cb % 2 == 0:
-                    nc.scalar.activation(result[:], o_ps[:], ACT.Relu, scale=g)
-                else:
-                    nc.vector.tensor_scalar(result[:], o_ps[:], g, 0.0, ALU.mult, ALU.max)
+                nc.scalar.activation(result[:], o_ps[:], ACT.Relu, scale=g)
                 first_column = t * PLACES + nh * BANK
                 nc.sync.dma_start(out[block(cb), first_column : first_column + BANK], result[:])
 
@@ -159,10 +155,8 @@ def tile_differentialgcnblock_b_kernel(tc, x, adj, w_intra, w_inter, offs, out):
                 nc.vector.tensor_scalar(
                     unused[:], adj_sb[pair][:, i, :], 1.0, None, ALU.mult, ALU.add, accum_out=degree[:, i : i + 1]
                 )
-            root = held.tile([PART, 2], F32, name=f"root{pair}")
-            nc.scalar.activation(root[:], degree[:], ACT.Sqrt)
             dinv.append(held.tile([PART, 2], F32, name=f"dinv{pair}"))
-            nc.vector.reciprocal(dinv[pair][:], root[:])
+            nc.scalar.activation(dinv[pair][:], degree[:], ACT.Abs_reciprocal_sqrt)
 
         project(0)
 

@@ -60,8 +60,9 @@ def tile_differentialgcnblock_b_kernel(tc, x, adj, w_intra, w_inter, offs, out):
             for kb in range(CHANNEL_BLOCKS):
                 nc.sync.dma_start(x_sb[t][kb][:], x[t, block(kb), :])
 
-        load_frame(0)
+        nc.sync.dma_start(x_sb[0][0][:], x[0, block(0), :])
         nc.sync.dma_start(w_intra_sb[:], w_intra.rearrange("(kb p) c -> p kb c", p=PART))
+        nc.sync.dma_start(x_sb[0][1][:], x[0, block(1), :])
         for pair in range(PAIRS):
             rows = slice(pair * PAIR_PLACES, (pair + 1) * PAIR_PLACES)
             nc.sync.dma_start(adj_sb[pair][:], adj[rows, :].rearrange("(i p) n -> p i n", p=PART))
@@ -76,46 +77,62 @@ def tile_differentialgcnblock_b_kernel(tc, x, adj, w_intra, w_inter, offs, out):
         inner = [[held.tile([PART, BANK], F32, name=f"inner{cb}_{nh}") for nh in range(PLACE_HALVES)] for cb in range(CHANNEL_BLOCKS)]
         y = [[[held.tile([PART, BANK], BF16, name=f"y{t}_{cb}_{nh}") for nh in range(PLACE_HALVES)] for cb in range(CHANNEL_BLOCKS)] for t in range(FRAMES)]
 
+        def look_up(t, kb, pair):
+            first_column = (t * PAIRS + pair) * PIECE_COLUMNS
+            piece = offsets[:, first_column : first_column + PIECE_COLUMNS]
+            picked = ring.tile([PART, PAIR_PLACES], F32, name="picked", bufs=8)
+            nc.scalar.activation(picked[:], x_sb[t][kb][:].indirect(piece), ACT.Copy)
+            nc.vector.tensor_copy(picked_bf[t][kb][pair][:], picked[:])
+
         def pick(t):
-            for pair in range(PAIRS):
-                first_column = (t * PAIRS + pair) * PIECE_COLUMNS
-                piece = offsets[:, first_column : first_column + PIECE_COLUMNS]
+            for kb in range(CHANNEL_BLOCKS):
+                for pair in range(PAIRS):
+                    look_up(t, kb, pair)
+
+        def project_pair(t, pair):
+            q_ps = psum.tile([PART, 2, CHANNELS], F32, name="q_ps", tag="bank")
+            for i in range(2):
                 for kb in range(CHANNEL_BLOCKS):
-                    picked = ring.tile([PART, PAIR_PLACES], F32, name="picked", bufs=8)
-                    nc.scalar.activation(picked[:], x_sb[t][kb][:].indirect(piece), ACT.Copy)
-                    nc.vector.tensor_copy(picked_bf[t][kb][pair][:], picked[:])
+                    nc.tensor.matmul(
+                        q_ps[:, i, :],
+                        lhsT=picked_bf[t][kb][pair][:, block(i)],
+                        rhs=w_intra_sb[:, kb, :],
+                        start=kb == 0,
+                        stop=kb == CHANNEL_BLOCKS - 1,
+                    )
+            return q_ps
+
+        def scale_pair(t, pair, q_ps):
+            for i in range(2):
+                nc.scalar.activation(q_t[t][pair][:, i, :], q_ps[:, i, :], ACT.Identity, scale=dinv[pair][:, i : i + 1])
 
         def project(t):
             for pair in range(PAIRS):
-                q_ps = psum.tile([PART, 2, CHANNELS], F32, name="q_ps", tag="bank")
-                for i in range(2):
-                    for kb in range(CHANNEL_BLOCKS):
-                        nc.tensor.matmul(
-                            q_ps[:, i, :],
-                            lhsT=picked_bf[t][kb][pair][:, block(i)],
-                            rhs=w_intra_sb[:, kb, :],
-                            start=kb == 0,
-                            stop=kb == CHANNEL_BLOCKS - 1,
-                        )
-                for i in range(2):
-                    nc.scalar.activation(q_t[t][pair][:, i, :], q_ps[:, i, :], ACT.Identity, scale=dinv[pair][:, i : i + 1])
+                scale_pair(t, pair, project_pair(t, pair))
 
-        def aggregate(t, nh):
-            z_ps = [psum.tile([PART, BANK], F32, name=f"z_ps{cb}", tag="bank") for cb in range(CHANNEL_BLOCKS)]
-            for pair in range(PAIRS):
-                for i in range(2):
-                    for cb in range(CHANNEL_BLOCKS):
-                        nc.tensor.matmul(
-                            z_ps[cb][:],
-                            lhsT=q_t[t][pair][:, i, block(cb)],
-                            rhs=adj_sb[pair][:, i, nh * BANK : (nh + 1) * BANK],
-                            start=pair == 0 and i == 0,
-                            stop=pair == PAIRS - 1 and i == 1,
-                        )
-            if t == 0:
-                spread_dinv(nh)
+        def open_half():
+            return [psum.tile([PART, BANK], F32, name=f"z_ps{cb}", tag="bank") for cb in range(CHANNEL_BLOCKS)]
+
+        def aggregate_pair(t, pair, nh, z_ps):
+            for i in range(2):
+                for cb in range(CHANNEL_BLOCKS):
+                    nc.tensor.matmul(
+                        z_ps[cb][:],
+                        lhsT=q_t[t][pair][:, i, block(cb)],
+                        rhs=adj_sb[pair][:, i, nh * BANK : (nh + 1) * BANK],
+                        start=pair == 0 and i == 0,
+                        stop=pair == PAIRS - 1 and i == 1,
+                    )
+
+        def rectify(t, nh, z_ps):
             for cb in range(CHANNEL_BLOCKS):
                 nc.vector.scalar_tensor_tensor(h[t][cb][nh][:], z_ps[cb][:], 0.0, dinv_row[FRAME_DEGREE[t]][nh][:], ALU.max, ALU.mult)
+
+        def aggregate(t, nh):
+            z_ps = open_half()
+            for pair in range(PAIRS):
+                aggregate_pair(t, pair, nh, z_ps)
+            rectify(t, nh, z_ps)
 
         def mix(t, nh):
             for cb in range(CHANNEL_BLOCKS):
@@ -145,20 +162,16 @@ def tile_differentialgcnblock_b_kernel(tc, x, adj, w_intra, w_inter, offs, out):
                 first_column = t * PLACES + nh * BANK
                 nc.sync.dma_start(out[block(cb), first_column : first_column + BANK], result[:])
 
-        pick(0)
+        dinv = [held.tile([PART, 2], F32, name=f"dinv{pair}") for pair in range(PAIRS)]
 
-        dinv = []
-        for pair in range(PAIRS):
+        def invert_degrees(pair):
             degree = held.tile([PART, 2], F32, name=f"degree{pair}")
             for i in range(2):
                 unused = ring.tile([PART, PLACES], BF16, name="unused")
                 nc.vector.tensor_scalar(
                     unused[:], adj_sb[pair][:, i, :], 1.0, None, ALU.mult, ALU.add, accum_out=degree[:, i : i + 1]
                 )
-            dinv.append(held.tile([PART, 2], F32, name=f"dinv{pair}"))
             nc.scalar.activation(dinv[pair][:], degree[:], ACT.Abs_reciprocal_sqrt)
-
-        project(0)
 
         identity = held.tile([PART, PART], F32, name="identity")
         make_identity(nc, identity[:])
@@ -174,8 +187,22 @@ def tile_differentialgcnblock_b_kernel(tc, x, adj, w_intra, w_inter, offs, out):
             for d in dinv_row:
                 nc.vector.tensor_scalar(dinv_row[d][nh][:], row_ps[:], 1.0 / math.sqrt(d), None, ALU.mult)
 
+        pick(0)
+        q_ps_of = [project_pair(0, pair) for pair in range(PAIRS)]
+        z_first = [open_half() for nh in range(PLACE_HALVES)]
+        for pair in range(PAIRS):
+            invert_degrees(pair)
+            scale_pair(0, pair, q_ps_of[pair])
+            for nh in range(PLACE_HALVES):
+                aggregate_pair(0, pair, nh, z_first[nh])
+        pick(1)
+        for nh in range(PLACE_HALVES):
+            spread_dinv(nh)
+            rectify(0, nh, z_first[nh])
+        project(1)
+
         summed = []
-        for t in range(FRAMES):
+        for t in range(1, FRAMES):
             if t + 1 < FRAMES:
                 pick(t + 1)
             for nh in range(PLACE_HALVES):

@@ -71,23 +71,24 @@ def tile_differentialgcnblock_b_kernel(tc, x, adj, w_intra, w_inter, offs, out):
         load_frame(2)
         load_frame(3)
 
-        picked_bf = [[[held.tile([PART, PAIR_PLACES], BF16, name=f"picked_bf{t}_{kb}_{pair}") for pair in range(PAIRS)] for kb in range(CHANNEL_BLOCKS)] for t in range(FRAMES)]
+        picked_bf = [[held.tile([PART, PLACES], BF16, name=f"picked_bf{t}_{kb}") for kb in range(CHANNEL_BLOCKS)] for t in range(FRAMES)]
         q_t = [[held.tile([PART, 2, CHANNELS], BF16, name=f"q_t{t}_{pair}") for pair in range(PAIRS)] for t in range(FRAMES)]
         h = [[[held.tile([PART, BANK], F32, name=f"h{t}_{cb}_{nh}") for nh in range(PLACE_HALVES)] for cb in range(CHANNEL_BLOCKS)] for t in range(FRAMES)]
         inner = [[held.tile([PART, BANK], F32, name=f"inner{cb}_{nh}") for nh in range(PLACE_HALVES)] for cb in range(CHANNEL_BLOCKS)]
         y = [[[held.tile([PART, BANK], BF16, name=f"y{t}_{cb}_{nh}") for nh in range(PLACE_HALVES)] for cb in range(CHANNEL_BLOCKS)] for t in range(FRAMES)]
 
-        def look_up(t, kb, pair):
-            first_column = (t * PAIRS + pair) * PIECE_COLUMNS
-            piece = offsets[:, first_column : first_column + PIECE_COLUMNS]
-            picked = ring.tile([PART, PAIR_PLACES], F32, name="picked", bufs=8)
+        def look_up(t, kb, first_pair, pairs):
+            first_column = (t * PAIRS + first_pair) * PIECE_COLUMNS
+            piece = offsets[:, first_column : first_column + pairs * PIECE_COLUMNS]
+            picked = ring.tile([PART, pairs * PAIR_PLACES], F32, name=f"picked{pairs}", bufs=8 // pairs)
             nc.scalar.activation(picked[:], x_sb[t][kb][:].indirect(piece), ACT.Copy)
-            nc.vector.tensor_copy(picked_bf[t][kb][pair][:], picked[:])
+            places = slice(first_pair * PAIR_PLACES, (first_pair + pairs) * PAIR_PLACES)
+            nc.vector.tensor_copy(picked_bf[t][kb][:, places], picked[:])
 
         def pick(t):
             for kb in range(CHANNEL_BLOCKS):
                 for pair in range(PAIRS):
-                    look_up(t, kb, pair)
+                    look_up(t, kb, pair, 1)
 
         def project_pair(t, pair):
             q_ps = psum.tile([PART, 2, CHANNELS], F32, name="q_ps", tag="bank")
@@ -95,7 +96,7 @@ def tile_differentialgcnblock_b_kernel(tc, x, adj, w_intra, w_inter, offs, out):
                 for kb in range(CHANNEL_BLOCKS):
                     nc.tensor.matmul(
                         q_ps[:, i, :],
-                        lhsT=picked_bf[t][kb][pair][:, block(i)],
+                        lhsT=picked_bf[t][kb][:, block(2 * pair + i)],
                         rhs=w_intra_sb[:, kb, :],
                         start=kb == 0,
                         stop=kb == CHANNEL_BLOCKS - 1,
@@ -110,40 +111,31 @@ def tile_differentialgcnblock_b_kernel(tc, x, adj, w_intra, w_inter, offs, out):
             for pair in range(PAIRS):
                 scale_pair(t, pair, project_pair(t, pair))
 
-        def open_half():
-            return [psum.tile([PART, BANK], F32, name=f"z_ps{cb}", tag="bank") for cb in range(CHANNEL_BLOCKS)]
+        def open_bank():
+            return psum.tile([PART, BANK], F32, name="z_ps", tag="bank")
 
-        def aggregate_pair(t, pair, nh, z_ps):
+        def aggregate_pair(t, pair, nh, cb, z_ps):
             for i in range(2):
-                for cb in range(CHANNEL_BLOCKS):
-                    nc.tensor.matmul(
-                        z_ps[cb][:],
-                        lhsT=q_t[t][pair][:, i, block(cb)],
-                        rhs=adj_sb[pair][:, i, nh * BANK : (nh + 1) * BANK],
-                        start=pair == 0 and i == 0,
-                        stop=pair == PAIRS - 1 and i == 1,
-                    )
+                nc.tensor.matmul(
+                    z_ps[:],
+                    lhsT=q_t[t][pair][:, i, block(cb)],
+                    rhs=adj_sb[pair][:, i, nh * BANK : (nh + 1) * BANK],
+                    start=pair == 0 and i == 0,
+                    stop=pair == PAIRS - 1 and i == 1,
+                )
 
-        def rectify(t, nh, z_ps):
-            for cb in range(CHANNEL_BLOCKS):
-                nc.vector.scalar_tensor_tensor(h[t][cb][nh][:], z_ps[cb][:], 0.0, dinv_row[FRAME_DEGREE[t]][nh][:], ALU.max, ALU.mult)
+        def rectify(t, nh, cb, z_ps):
+            nc.vector.scalar_tensor_tensor(h[t][cb][nh][:], z_ps[:], 0.0, dinv_row[FRAME_DEGREE[t]][nh][:], ALU.max, ALU.mult)
 
-        def aggregate(t, nh):
-            z_ps = open_half()
-            for pair in range(PAIRS):
-                aggregate_pair(t, pair, nh, z_ps)
-            rectify(t, nh, z_ps)
-
-        def mix(t, nh):
-            for cb in range(CHANNEL_BLOCKS):
-                if t == INNER[0]:
-                    nc.vector.tensor_tensor(inner[cb][nh][:], h[INNER[0]][cb][nh][:], h[INNER[1]][cb][nh][:], ALU.add)
-                if t in INNER:
-                    (outer,) = [u for u in neighbours(t) if u not in INNER]
-                    nc.vector.tensor_tensor(y[t][cb][nh][:], inner[cb][nh][:], h[outer][cb][nh][:], ALU.add)
-                else:
-                    a, b = neighbours(t)
-                    nc.vector.tensor_tensor(y[t][cb][nh][:], h[a][cb][nh][:], h[b][cb][nh][:], ALU.add)
+        def mix(t, nh, cb):
+            if t == INNER[0]:
+                nc.vector.tensor_tensor(inner[cb][nh][:], h[INNER[0]][cb][nh][:], h[INNER[1]][cb][nh][:], ALU.add)
+            if t in INNER:
+                (outer,) = [u for u in neighbours(t) if u not in INNER]
+                nc.vector.tensor_tensor(y[t][cb][nh][:], inner[cb][nh][:], h[outer][cb][nh][:], ALU.add)
+            else:
+                a, b = neighbours(t)
+                nc.vector.tensor_tensor(y[t][cb][nh][:], h[a][cb][nh][:], h[b][cb][nh][:], ALU.add)
 
         def project_out(t, nh):
             g = 1.0 / math.sqrt(FRAME_DEGREE[t])
@@ -187,18 +179,24 @@ def tile_differentialgcnblock_b_kernel(tc, x, adj, w_intra, w_inter, offs, out):
             for d in dinv_row:
                 nc.vector.tensor_scalar(dinv_row[d][nh][:], row_ps[:], 1.0 / math.sqrt(d), None, ALU.mult)
 
-        pick(0)
-        q_ps_of = [project_pair(0, pair) for pair in range(PAIRS)]
-        z_first = [open_half() for nh in range(PLACE_HALVES)]
+        look_up(0, 0, 0, PAIRS)
+        q_ps_of = []
+        for pair in range(PAIRS):
+            look_up(0, 1, pair, 1)
+            q_ps_of.append(project_pair(0, pair))
+        z_first = [[open_bank() for cb in range(CHANNEL_BLOCKS)] for nh in range(PLACE_HALVES)]
         for pair in range(PAIRS):
             invert_degrees(pair)
             scale_pair(0, pair, q_ps_of[pair])
+            if (pair + 1) % PAIRS_IN_HALF == 0:
+                spread_dinv(pair // PAIRS_IN_HALF)
             for nh in range(PLACE_HALVES):
-                aggregate_pair(0, pair, nh, z_first[nh])
+                for cb in range(CHANNEL_BLOCKS):
+                    aggregate_pair(0, pair, nh, cb, z_first[nh][cb])
         pick(1)
         for nh in range(PLACE_HALVES):
-            spread_dinv(nh)
-            rectify(0, nh, z_first[nh])
+            for cb in range(CHANNEL_BLOCKS):
+                rectify(0, nh, cb, z_first[nh][cb])
         project(1)
 
         summed = []
@@ -206,11 +204,15 @@ def tile_differentialgcnblock_b_kernel(tc, x, adj, w_intra, w_inter, offs, out):
             if t + 1 < FRAMES:
                 pick(t + 1)
             for nh in range(PLACE_HALVES):
-                aggregate(t, nh)
                 summed_before = summed
                 summed = [(u, nh) for u in range(FRAMES) if neighbours(u)[-1] == t]
-                for u, uh in summed:
-                    mix(u, uh)
+                for cb in range(CHANNEL_BLOCKS):
+                    z_ps = open_bank()
+                    for pair in range(PAIRS):
+                        aggregate_pair(t, pair, nh, cb, z_ps)
+                    rectify(t, nh, cb, z_ps)
+                    for u, uh in summed:
+                        mix(u, uh, cb)
                 if nh == PLACE_HALVES - 1 and t + 1 < FRAMES:
                     project(t + 1)
                 for u, uh in summed_before:

@@ -172,10 +172,9 @@ def tile_differentialgcnblock_b_kernel(tc, x, adj, w_intra, w_inter, offs, out):
         def spread_dinv(nh):
             row_ps = psum.tile([PART, BANK], F32, name="row_ps", tag="bank")
             for j in range(PAIRS_IN_HALF):
-                spread = ring.tile([PART, 2, PART], F32, name="spread")
-                nc.gpsimd.tensor_copy(spread[:], dinv[nh * PAIRS_IN_HALF + j][:].unsqueeze(2).to_broadcast([PART, 2, PART]))
                 for i in range(2):
-                    nc.tensor.transpose(row_ps[:, block(2 * j + i)], spread[:, i, :], identity[:])
+                    column = dinv[nh * PAIRS_IN_HALF + j][:, i : i + 1]
+                    nc.tensor.transpose(row_ps[:, block(2 * j + i)], column.to_broadcast([PART, PART]), identity[:])
             for d in dinv_row:
                 nc.vector.tensor_scalar(dinv_row[d][nh][:], row_ps[:], 1.0 / math.sqrt(d), None, ALU.mult)
 

import math

import concourse.mybir as mybir
from concourse.masks import make_identity

F32 = mybir.dt.float32
BF16 = mybir.dt.bfloat16
U16 = mybir.dt.uint16
ACT = mybir.ActivationFunctionType
ALU = mybir.AluOpType

FRAMES = 4
CHANNELS = 256
NODES = 2048
PLACES = 1024
PART = 128
BANK = 512
CHANNEL_BLOCKS = CHANNELS // PART
PLACE_HALVES = PLACES // BANK
PAIRS = PLACES // (2 * PART)
PAIRS_IN_HALF = PAIRS // PLACE_HALVES
PAIR_PLACES = 2 * PART
PIECE_COLUMNS = PAIR_PLACES // 16
FRAME_DEGREE = (2, 3, 3, 2)

FLOPS = 2 * FRAMES * (PLACES * PLACES * CHANNELS + 2 * CHANNELS * CHANNELS * PLACES)


def neighbours(t):
    return [u for u in (t - 1, t, t + 1) if 0 <= u < FRAMES]


INNER = (1, 2)


def block(i):
    return slice(i * PART, (i + 1) * PART)


def tile_differentialgcnblock_b_kernel(tc, x, adj, w_intra, w_inter, offs, out):
    nc = tc.nc
    with (
        tc.tile_pool(name="held", bufs=1) as held,
        tc.tile_pool(name="ring", bufs=4) as ring,
        tc.psum_pool(name="psum", bufs=8) as psum,
    ):
        one = held.tile([PART, 1], F32, name="one")
        nc.vector.memset(one[:], 1.0)
        root_of_one = held.tile([PART, 1], F32, name="root_of_one")
        nc.scalar.activation(root_of_one[:], one[:], ACT.Abs_reciprocal_sqrt)

        offsets = held.tile([PART, FRAMES * PAIRS * PIECE_COLUMNS], U16, name="offsets")
        nc.sync.dma_start(offsets[:], offs)
        x_sb = [[held.tile([PART, NODES], F32, name=f"x{t}_{kb}") for kb in range(CHANNEL_BLOCKS)] for t in range(FRAMES)]
        adj_sb = [held.tile([PART, 2, PLACES], BF16, name=f"adj{pair}") for pair in range(PAIRS)]
        w_intra_sb = held.tile([PART, CHANNEL_BLOCKS, CHANNELS], BF16, name="w_intra_sb")
        w_inter_sb = held.tile([PART, CHANNEL_BLOCKS, CHANNELS], BF16, name="w_inter_sb")

        def load_frame(t):
            for kb in range(CHANNEL_BLOCKS):
                nc.sync.dma_start(x_sb[t][kb][:], x[t, block(kb), :])

        nc.sync.dma_start(x_sb[0][0][:], x[0, block(0), :])
        nc.sync.dma_start(w_intra_sb[:], w_intra.rearrange("(kb p) c -> p kb c", p=PART))
        nc.sync.dma_start(x_sb[0][1][:], x[0, block(1), :])
        for pair in range(PAIRS):
            rows = slice(pair * PAIR_PLACES, (pair + 1) * PAIR_PLACES)
            nc.sync.dma_start(adj_sb[pair][:], adj[rows, :].rearrange("(i p) n -> p i n", p=PART))
        load_frame(1)
        nc.sync.dma_start(w_inter_sb[:], w_inter.rearrange("(kb p) c -> p kb c", p=PART))
        load_frame(2)
        load_frame(3)

        picked_bf = [[held.tile([PART, PLACES], BF16, name=f"picked_bf{t}_{kb}") for kb in range(CHANNEL_BLOCKS)] for t in range(FRAMES)]
        q_t = [[held.tile([PART, 2, CHANNELS], BF16, name=f"q_t{t}_{pair}") for pair in range(PAIRS)] for t in range(FRAMES)]
        h = [[[held.tile([PART, BANK], F32, name=f"h{t}_{cb}_{nh}") for nh in range(PLACE_HALVES)] for cb in range(CHANNEL_BLOCKS)] for t in range(FRAMES)]
        inner = [[held.tile([PART, BANK], F32, name=f"inner{cb}_{nh}") for nh in range(PLACE_HALVES)] for cb in range(CHANNEL_BLOCKS)]
        y = [[[held.tile([PART, BANK], BF16, name=f"y{t}_{cb}_{nh}") for nh in range(PLACE_HALVES)] for cb in range(CHANNEL_BLOCKS)] for t in range(FRAMES)]

        def look_up(t, kb, first_pair, pairs):
            first_column = (t * PAIRS + first_pair) * PIECE_COLUMNS
            piece = offsets[:, first_column : first_column + pairs * PIECE_COLUMNS]
            picked = ring.tile([PART, pairs * PAIR_PLACES], F32, name=f"picked{pairs}", bufs=8 // pairs)
            nc.scalar.activation(picked[:], x_sb[t][kb][:].indirect(piece), ACT.Copy)
            places = slice(first_pair * PAIR_PLACES, (first_pair + pairs) * PAIR_PLACES)
            nc.vector.tensor_copy(picked_bf[t][kb][:, places], picked[:])

        def pick(t):
            for kb in range(CHANNEL_BLOCKS):
                for pair in range(PAIRS):
                    look_up(t, kb, pair, 1)

        def project_pair(t, pair):
            q_ps = psum.tile([PART, 2, CHANNELS], F32, name="q_ps", tag="bank")
            for i in range(2):
                for kb in range(CHANNEL_BLOCKS):
                    nc.tensor.matmul(
                        q_ps[:, i, :],
                        lhsT=picked_bf[t][kb][:, block(2 * pair + i)],
                        rhs=w_intra_sb[:, kb, :],
                        start=kb == 0,
                        stop=kb == CHANNEL_BLOCKS - 1,
                    )
            return q_ps

        def scale_pair(t, pair, q_ps):
            for i in range(2):
                nc.scalar.activation(q_t[t][pair][:, i, :], q_ps[:, i, :], ACT.Identity, scale=dinv[pair][:, i : i + 1])

        def project(t):
            for pair in range(PAIRS):
                scale_pair(t, pair, project_pair(t, pair))

        def open_bank():
            return psum.tile([PART, BANK], F32, name="z_ps", tag="bank")

        def aggregate_pair(t, pair, nh, cb, z_ps):
            for i in range(2):
                nc.tensor.matmul(
                    z_ps[:],
                    lhsT=q_t[t][pair][:, i, block(cb)],
                    rhs=adj_sb[pair][:, i, nh * BANK : (nh + 1) * BANK],
                    start=pair == 0 and i == 0,
                    stop=pair == PAIRS - 1 and i == 1,
                )

        def rectify(t, nh, cb, z_ps):
            nc.vector.scalar_tensor_tensor(h[t][cb][nh][:], z_ps[:], 0.0, dinv_row[FRAME_DEGREE[t]][nh][:], ALU.max, ALU.mult)

        def mix(t, nh, cb):
            if t == INNER[0]:
                nc.vector.tensor_tensor(inner[cb][nh][:], h[INNER[0]][cb][nh][:], h[INNER[1]][cb][nh][:], ALU.add)
            if t in INNER:
                (outer,) = [u for u in neighbours(t) if u not in INNER]
                nc.vector.tensor_tensor(y[t][cb][nh][:], inner[cb][nh][:], h[outer][cb][nh][:], ALU.add)
            else:
                a, b = neighbours(t)
                nc.vector.tensor_tensor(y[t][cb][nh][:], h[a][cb][nh][:], h[b][cb][nh][:], ALU.add)

        def project_out(t, nh):
            g = 1.0 / math.sqrt(FRAME_DEGREE[t])
            for cb in range(CHANNEL_BLOCKS):
                o_ps = psum.tile([PART, BANK], F32, name="o_ps", tag="bank")
                for kb in range(CHANNEL_BLOCKS):
                    nc.tensor.matmul(
                        o_ps[:],
                        lhsT=w_inter_sb[:, kb, block(cb)],
                        rhs=y[t][kb][nh][:],
                        start=kb == 0,
                        stop=kb == CHANNEL_BLOCKS - 1,
                    )
                result = ring.tile([PART, BANK], F32, name="result", bufs=8)
                nc.scalar.activation(result[:], o_ps[:], ACT.Relu, scale=g)
                first_column = t * PLACES + nh * BANK
                nc.sync.dma_start(out[block(cb), first_column : first_column + BANK], result[:])

        dinv = [held.tile([PART, 2], F32, name=f"dinv{pair}") for pair in range(PAIRS)]

        def invert_degrees(pair):
            degree = held.tile([PART, 2], F32, name=f"degree{pair}")
            for i in range(2):
                unused = ring.tile([PART, PLACES], BF16, name="unused")
                nc.vector.tensor_scalar(
                    unused[:], adj_sb[pair][:, i, :], 1.0, None, ALU.mult, ALU.add, accum_out=degree[:, i : i + 1]
                )
            nc.scalar.activation(dinv[pair][:], degree[:], ACT.Abs_reciprocal_sqrt)

        identity = held.tile([PART, PART], F32, name="identity")
        make_identity(nc, identity[:])
        dinv_row = {d: [held.tile([PART, BANK], F32, name=f"dinv_row{d}_{nh}") for nh in range(PLACE_HALVES)] for d in sorted(set(FRAME_DEGREE))}

        def spread_dinv(nh):
            row_ps = psum.tile([PART, BANK], F32, name="row_ps", tag="bank")
            for j in range(PAIRS_IN_HALF):
                for i in range(2):
                    column = dinv[nh * PAIRS_IN_HALF + j][:, i : i + 1]
                    nc.tensor.transpose(row_ps[:, block(2 * j + i)], column.to_broadcast([PART, PART]), identity[:])
            for d in dinv_row:
                nc.vector.tensor_scalar(dinv_row[d][nh][:], row_ps[:], 1.0 / math.sqrt(d), None, ALU.mult)

        look_up(0, 0, 0, PAIRS)
        q_ps_of = []
        for pair in range(PAIRS):
            look_up(0, 1, pair, 1)
            q_ps_of.append(project_pair(0, pair))
        z_first = [[open_bank() for cb in range(CHANNEL_BLOCKS)] for nh in range(PLACE_HALVES)]
        for pair in range(PAIRS):
            invert_degrees(pair)
            scale_pair(0, pair, q_ps_of[pair])
            if (pair + 1) % PAIRS_IN_HALF == 0:
                spread_dinv(pair // PAIRS_IN_HALF)
            for nh in range(PLACE_HALVES):
                for cb in range(CHANNEL_BLOCKS):
                    aggregate_pair(0, pair, nh, cb, z_first[nh][cb])
        pick(1)
        for nh in range(PLACE_HALVES):
            for cb in range(CHANNEL_BLOCKS):
                rectify(0, nh, cb, z_first[nh][cb])
        project(1)

        summed = []
        for t in range(1, FRAMES):
            if t + 1 < FRAMES:
                pick(t + 1)
            for nh in range(PLACE_HALVES):
                summed_before = summed
                summed = [(u, nh) for u in range(FRAMES) if neighbours(u)[-1] == t]
                for cb in range(CHANNEL_BLOCKS):
                    z_ps = open_bank()
                    for pair in range(PAIRS):
                        aggregate_pair(t, pair, nh, cb, z_ps)
                    rectify(t, nh, cb, z_ps)
                    for u, uh in summed:
                        mix(u, uh, cb)
                if nh == PLACE_HALVES - 1 and t + 1 < FRAMES:
                    project(t + 1)
                for u, uh in summed_before:
                    project_out(u, uh)
        for u, uh in summed:
            project_out(u, uh)
